import numpy as np
import ml_dtypes


def mxq(x, axis, fmt="e4m3"):
    dtype, down = {"e4m3": (ml_dtypes.float8_e4m3fn, 7), "e5m2": (ml_dtypes.float8_e5m2, 14)}[fmt]
    v = np.moveaxis(np.asarray(x, np.float32).astype(ml_dtypes.bfloat16).astype(np.float64), axis, -1)
    blocks = v.reshape(v.shape[:-1] + (-1, 32))
    amax = np.abs(blocks).max(-1, keepdims=True)
    byte = np.maximum(np.where(amax > 0, np.frexp(amax)[1] - 1 + 127, 0) - down, 1)
    scale = np.exp2(byte - 127.0)
    codes = (blocks / scale).astype(np.float32).astype(dtype).astype(np.float64)
    return np.moveaxis((codes * scale).reshape(v.shape), -1, axis)


WIDE = False


def mx_kscale(k):
    if not WIDE:
        return np.ones(k)
    levels = np.array([10, -10, 5, -5, 0])
    if k % 512:
        return np.exp2(np.random.permutation(np.resize(levels, k // 32))).repeat(32)
    a = np.empty((k // 512, 16))
    for p in range(k // 512):
        a[p, :8] = np.random.permutation(np.resize(levels, 8))
        for g in range(8):
            far = levels[np.abs(levels - a[p, g]) >= 10]
            a[p, g + 8] = far[np.random.randint(len(far))]
    return np.exp2(a.ravel()).repeat(32)


BF16 = ml_dtypes.bfloat16


def bf(x):
    return np.asarray(x, np.float32).astype(BF16)


def f64(x):
    return np.asarray(x).astype(np.float64)


B, T, N, DH, D = 1, 128, 4, 128, 512
KC = N * DH


def setup_inputs():
    r = np.random.standard_normal
    s = mx_kscale(D)
    t = mx_kscale(KC).reshape(N, DH)
    return {"normalized_resid_pre": bf(r((B, T, D)) * s),
            "W_C": bf(r((N, D, DH)) / np.sqrt(D) / s[None, :, None] * t[:, None, :]),
            "b_C": bf(0.1 * r((N, DH)) * t),
            "W_K": bf(1.3 / np.sqrt(KC) * r((N, DH, DH, DH)) / t[:, None, None, :])}


def reference(normalized_resid_pre, W_C, b_C, W_K):
    x = f64(normalized_resid_pre)
    wc = f64(W_C).transpose(1, 0, 2).reshape(D, KC)
    c = (mxq(x, 2, "e4m3") @ mxq(wc, 0, "e4m3")) + f64(b_C).reshape(KC)
    wk = f64(W_K).transpose(0, 3, 1, 2).reshape(KC, DH * DH)
    step1 = mxq(c, 2, "e4m3") @ mxq(wk, 0, "e4m3")
    return step1.reshape(B, T, DH, DH)

@@ -1,0 +1,165 @@
+from contextlib import ExitStack
+
+import concourse.mybir as mybir
+from concourse.masks import make_identity
+
+F32 = mybir.dt.float32
+BF16 = mybir.dt.bfloat16
+U32 = mybir.dt.uint32
+U8 = mybir.dt.uint8
+FP8X4 = mybir.dt.float8_e4m3fn_x4
+ADD = mybir.AluOpType.add
+
+P = 128
+T = 128
+D = 512
+NH = 4
+DH = 128
+KC = NH * DH
+ROWS = DH * DH
+FLOPS = 2 * T * D * KC + 2 * T * KC * ROWS
+
+BANK_DT = F32
+M_LIST = [4,4,8,16,16,16,16,16,16,8,4,4]
+PRELOAD = 5
+LOADS_AFTER_STORE = {2: (5,), 3: (6,), 4: (7,), 5: (8,), 6: (9, 10, 11)}
+GS = 4
+
+
+def tile_trittentioncube_pa_kernel(tc, normalized_resid_pre, W_C, b_C, W_K, out):
+    nc = tc.nc
+    assert sum(M_LIST) == DH
+    x_dram = normalized_resid_pre.rearrange("b r d -> (b r) d")
+    out_dram = out.rearrange("b r i j -> (b r) (i j)")
+    wk_dram = W_K.rearrange("n i j k -> n (i j) k")
+
+    with ExitStack() as ctx:
+        keep = ctx.enter_context(tc.tile_pool(name="keep", bufs=1))
+        rawp = ctx.enter_context(tc.tile_pool(name="rawp", bufs=1))
+        ordp = ctx.enter_context(tc.tile_pool(name="ordp", bufs=3))
+        grpp = ctx.enter_context(tc.tile_pool(name="grpp", bufs=3))
+        codp = ctx.enter_context(tc.tile_pool(name="codp", bufs=3))
+        stgp = ctx.enter_context(tc.tile_pool(name="stgp", bufs=4))
+        tpp = ctx.enter_context(tc.psum_pool(name="tpp", bufs=6))
+        accp = ctx.enter_context(tc.psum_pool(name="accp", bufs=2))
+        ctx.enter_context(tc.manual_schedule(engines={mybir.EngineType.SP}))
+
+        x_sb = keep.tile([P, D], BF16, name="x_sb")
+        nc.sync.dma_start(out=x_sb[:], in_=x_dram)
+        wc_raw = keep.tile([P, NH, 4 * DH], BF16, name="wc_raw")
+        nc.sync.dma_start(out=wc_raw[:], in_=W_C.rearrange("n (p j) k -> p n (j k)", j=4))
+        b_sb = keep.tile([P, 4], BF16, name="b_sb")
+        nc.sync.dma_start(out=b_sb[:], in_=b_C.rearrange("n (q t) -> (n q) t", t=4))
+        raws = []
+        row0 = 0
+        for c, m in enumerate(M_LIST):
+            raw = rawp.tile([P, NH, m * DH], BF16, name="raw%d" % c)
+            raws.append((raw, m, row0))
+            row0 += P * m
+
+        def load(c):
+            raw, m, row0 = raws[c]
+            nc.sync.dma_start(
+                out=raw[:],
+                in_=wk_dram[:, row0 : row0 + P * m, :].rearrange("n (p s) k -> p n (s k)", s=m),
+            )
+
+        for c in range(PRELOAD):
+            load(c)
+
+        ident = keep.tile([P, P], F32, name="ident")
+        make_identity(nc, ident[:])
+        warm = keep.tile([P, 8], F32, name="warm")
+        nc.scalar.copy(out=warm[:], in_=ident[:, 0:8])
+
+        xw = x_sb[:].bitcast(F32)
+        xt = tpp.tile([P, 4, P], F32, name="xt", tag="tp")
+        for u in range(2):
+            nc.tensor.transpose(xt[:, u, :], xw[:, u : D // 2 : 2], ident[:])
+        x_g = keep.tile([P, 4 * T], BF16, name="x_g", align_bytes=64)
+        nc.vector.tensor_copy(
+            out=x_g[:].bitcast(F32).rearrange("q (r u) -> q r u", u=2),
+            in_=xt[:, 0:2, :].rearrange("q u r -> q r u"),
+        )
+        x_codes = keep.tile([P, T], U32, name="x_codes", align_bytes=64)
+        x_scales = keep.tile([P, T], U8, name="x_scales", align_bytes=64)
+        nc.vector.quantize_mx(out=x_codes[:].bitcast(FP8X4), scales=x_scales[:], in_=x_g[:])
+
+        wc_g = keep.tile([P, 4 * KC], BF16, name="wc_g", align_bytes=64)
+        wc_dst = wc_g[:].rearrange("p (t n q j) -> p t n q j", t=4, n=NH, q=32, j=4)
+        wc_src = wc_raw[:].rearrange("p n (j q t) -> p t n q j", j=4, q=32, t=4)
+        for t in range(4):
+            if t % 2 == 0:
+                nc.vector.tensor_copy(out=wc_dst[:, t], in_=wc_src[:, t])
+            else:
+                nc.scalar.copy(out=wc_dst[:, t], in_=wc_src[:, t])
+        wc_codes = keep.tile([P, KC], U32, name="wc_codes", align_bytes=64)
+        wc_scales = keep.tile([P, KC], U8, name="wc_scales", align_bytes=64)
+        nc.vector.quantize_mx(out=wc_codes[:].bitcast(FP8X4), scales=wc_scales[:], in_=wc_g[:])
+
+        c_ps = accp.tile([P, 4, T], BANK_DT, name="c_ps", tag="acc")
+        for t in range(4):
+            nc.tensor.matmul_mx(
+                out=c_ps[:, t, :],
+                lhsT=wc_codes[:, P * t : P * (t + 1)].bitcast(FP8X4),
+                lhsT_scale=wc_scales[:, P * t : P * (t + 1)],
+                rhs=x_codes[:].bitcast(FP8X4),
+                rhs_scale=x_scales[:],
+                start=True,
+                stop=True,
+            )
+        c_g = keep.tile([P, 4 * T], BF16, name="c_g", align_bytes=64)
+        nc.vector.tensor_tensor(
+            out=c_g[:].rearrange("q (r t) -> q r t", t=4),
+            in0=c_ps[:].rearrange("q t r -> q r t"),
+            in1=b_sb[:].unsqueeze(1).to_broadcast([P, T, 4]),
+            op=ADD,
+        )
+        c_codes = keep.tile([P, T], U32, name="c_codes", align_bytes=64)
+        c_scales = keep.tile([P, T], U8, name="c_scales", align_bytes=64)
+        nc.vector.quantize_mx(out=c_codes[:].bitcast(FP8X4), scales=c_scales[:], in_=c_g[:])
+
+        g = 0
+        for c, (raw, m, row0) in enumerate(raws):
+            raw_w = raw[:].rearrange("p n x -> p (n x)").bitcast(F32)
+            raw_v = raw_w.rearrange("p (n s w u) -> p s u n w", n=NH, s=m, w=32, u=2)
+            stg = stgp.tile([P, P * m], F32, name="stg", tag="stg")
+            stg_v = stg[:].rearrange("r (p s) -> r p s", s=m)
+            for sg in range(m // GS):
+                ordt = ordp.tile([P, GS, 2, P], F32, name="ordt", tag="ordt")
+                nc.vector.tensor_copy(
+                    out=ordt[:].rearrange("p s u (n w) -> p s u n w", n=NH),
+                    in_=raw_v[:, GS * sg : GS * (sg + 1), :, :, :],
+                )
+                grp = grpp.tile([P, 4 * 512], BF16, name="grp", tag="grp", align_bytes=64)
+                grp_w = grp[:].bitcast(F32)
+                for h in range(2):
+                    tp = tpp.tile([P, 4, P], F32, name="tp", tag="tp")
+                    for a in range(4):
+                        nc.tensor.transpose(tp[:, a, :], ordt[:, 2 * h + a // 2, a % 2, :], ident[:])
+                    dst = grp_w[:, 512 * h : 512 * (h + 1)].rearrange("q (p a) -> q p a", a=4)
+                    src = tp[:].rearrange("q a p -> q p a")
+                    nc.scalar.copy(out=dst, in_=src)
+                codes = codp.tile([P, 512], U32, name="codes", tag="codes", align_bytes=64)
+                scales = codp.tile([P, 512], U8, name="scales", tag="scales", align_bytes=64)
+                nc.vector.quantize_mx(out=codes[:].bitcast(FP8X4), scales=scales[:], in_=grp[:])
+                acc = accp.tile([P, 512], F32, name="acc", tag="acc")
+                nc.tensor.matmul_mx(
+                    out=acc[:],
+                    lhsT=c_codes[:].bitcast(FP8X4),
+                    lhsT_scale=c_scales[:],
+                    rhs=codes[:].bitcast(FP8X4),
+                    rhs_scale=scales[:],
+                    start=True,
+                    stop=True,
+                )
+                dst = stg_v[:, :, GS * sg : GS * (sg + 1)].rearrange("r p (h t) -> r p h t", h=2)
+                src = acc[:].rearrange("r (h p t) -> r p h t", h=2, t=2)
+                if g % 2 == 0:
+                    nc.vector.tensor_copy(out=dst, in_=src)
+                else:
+                    nc.scalar.copy(out=dst, in_=src)
+                g += 1
+            nc.sync.dma_start(out=out_dram[:, row0 : row0 + P * m], in_=stg[:])
+            for c2 in LOADS_AFTER_STORE.get(c, ()):
+                load(c2)

@@ -23,6 +23,8 @@ BANK_DT = F32
 M_LIST = [4,4,8,16,16,16,16,16,16,8,4,4]
 PRELOAD = 5
 LOADS_AFTER_STORE = {2: (5,), 3: (6,), 4: (7,), 5: (8,), 6: (9, 10, 11)}
+WARM_START = 8
+WARM_TWICE = 8
 GS = 4
 
 
@@ -74,6 +76,8 @@ def tile_trittentioncube_pa_kernel(tc, normalized_resid_pre, W_C, b_C, W_K, out)
 
         xw = x_sb[:].bitcast(F32)
         xt = tpp.tile([P, 4, P], F32, name="xt", tag="tp")
+        for i in range(WARM_START):
+            nc.tensor.matmul(out=xt[:, 2 + i % 2, :], lhsT=ident[:], rhs=ident[:], start=True, stop=True)
         for u in range(2):
             nc.tensor.transpose(xt[:, u, :], xw[:, u : D // 2 : 2], ident[:])
         x_g = keep.tile([P, 4 * T], BF16, name="x_g", align_bytes=64)
@@ -135,6 +139,8 @@ def tile_trittentioncube_pa_kernel(tc, normalized_resid_pre, W_C, b_C, W_K, out)
                 grp_w = grp[:].bitcast(F32)
                 for h in range(2):
                     tp = tpp.tile([P, 4, P], F32, name="tp", tag="tp")
+                    if h == 0 or g < WARM_TWICE:
+                        nc.tensor.matmul(out=tp[:, 0, :], lhsT=ident[:], rhs=ident[:], start=True, stop=True)
                     for a in range(4):
                         nc.tensor.transpose(tp[:, a, :], ordt[:, 2 * h + a // 2, a % 2, :], ident[:])
                     dst = grp_w[:, 512 * h : 512 * (h + 1)].rearrange("q (p a) -> q p a", a=4)

@@ -20,12 +20,15 @@ ROWS = DH * DH
 FLOPS = 2 * T * D * KC + 2 * T * KC * ROWS
 
 BANK_DT = F32
-M_LIST = [4,4,8,16,16,16,16,16,16,8,4,4]
-PRELOAD = 5
-LOADS_AFTER_STORE = {2: (5,), 3: (6,), 4: (7,), 5: (8,), 6: (9, 10, 11)}
-WARM_START = 8
-WARM_TWICE = 8
+M_LIST = [4,4,4,4,8,8,16,16,16,16,16,8,4,4]
 GS = 4
+LEAD = 6
+LAG_B = 2
+LAG_Q = 3
+LAG_D = 4
+WARM0 = 2
+WARM1 = 4
+WARM_TWICE = 8
 
 
 def tile_trittentioncube_pa_kernel(tc, normalized_resid_pre, W_C, b_C, W_K, out):
@@ -34,6 +37,16 @@ def tile_trittentioncube_pa_kernel(tc, normalized_resid_pre, W_C, b_C, W_K, out)
     x_dram = normalized_resid_pre.rearrange("b r d -> (b r) d")
     out_dram = out.rearrange("b r i j -> (b r) (i j)")
     wk_dram = W_K.rearrange("n i j k -> n (i j) k")
+
+    chunks = []
+    group_chunk = []
+    row0 = 0
+    for c, m in enumerate(M_LIST):
+        chunks.append((m, row0, len(group_chunk)))
+        for sg in range(m // GS):
+            group_chunk.append((c, sg))
+        row0 += P * m
+    ng = len(group_chunk)
 
     with ExitStack() as ctx:
         keep = ctx.enter_context(tc.tile_pool(name="keep", bufs=1))
@@ -44,42 +57,60 @@ def tile_trittentioncube_pa_kernel(tc, normalized_resid_pre, W_C, b_C, W_K, out)
         stgp = ctx.enter_context(tc.tile_pool(name="stgp", bufs=4))
         tpp = ctx.enter_context(tc.psum_pool(name="tpp", bufs=6))
         accp = ctx.enter_context(tc.psum_pool(name="accp", bufs=2))
-        ctx.enter_context(tc.manual_schedule(engines={mybir.EngineType.SP}))
+        ctx.enter_context(tc.manual_schedule())
+
+        raws = []
+        for c, m in enumerate(M_LIST):
+            raw = rawp.tile([P, NH, m * DH], BF16, name="raw%d" % c)
+            raws.append(raw)
+
+        def load(c):
+            m, row0, g0 = chunks[c]
+            nc.sync.dma_start(
+                out=raws[c][:],
+                in_=wk_dram[:, row0 : row0 + P * m, :].rearrange("n (p s) k -> p n (s k)", s=m),
+            )
+
+        def loads_of_step(i):
+            for c in range(len(chunks)):
+                first = max(chunks[c][2] - LEAD, 0)
+                if first == i:
+                    load(c)
+
+        def dummy(dst):
+            nc.tensor.matmul(out=dst, lhsT=ident[:], rhs=ident[:], start=True, stop=True)
 
         x_sb = keep.tile([P, D], BF16, name="x_sb")
         nc.sync.dma_start(out=x_sb[:], in_=x_dram)
         wc_raw = keep.tile([P, NH, 4 * DH], BF16, name="wc_raw")
         nc.sync.dma_start(out=wc_raw[:], in_=W_C.rearrange("n (p j) k -> p n (j k)", j=4))
-        b_sb = keep.tile([P, 4], BF16, name="b_sb")
-        nc.sync.dma_start(out=b_sb[:], in_=b_C.rearrange("n (q t) -> (n q) t", t=4))
-        raws = []
-        row0 = 0
-        for c, m in enumerate(M_LIST):
-            raw = rawp.tile([P, NH, m * DH], BF16, name="raw%d" % c)
-            raws.append((raw, m, row0))
-            row0 += P * m
-
-        def load(c):
-            raw, m, row0 = raws[c]
-            nc.sync.dma_start(
-                out=raw[:],
-                in_=wk_dram[:, row0 : row0 + P * m, :].rearrange("n (p s) k -> p n (s k)", s=m),
-            )
-
-        for c in range(PRELOAD):
-            load(c)
+        b_row = keep.tile([1, KC], BF16, name="b_row")
+        nc.sync.dma_start(out=b_row[:], in_=b_C.rearrange("(o n) k -> o (n k)", o=1))
+        loads_of_step(0)
 
         ident = keep.tile([P, P], F32, name="ident")
         make_identity(nc, ident[:])
+        b_pad = keep.tile([P, KC], F32, name="b_pad")
+        nc.gpsimd.memset(b_pad[:], 0.0)
         warm = keep.tile([P, 8], F32, name="warm")
         nc.scalar.copy(out=warm[:], in_=ident[:, 0:8])
 
+        wt = tpp.tile([P, 4, P], F32, name="wt", tag="tp")
+        for i in range(WARM0):
+            dummy(wt[:, i % 4, :])
         xw = x_sb[:].bitcast(F32)
         xt = tpp.tile([P, 4, P], F32, name="xt", tag="tp")
-        for i in range(WARM_START):
-            nc.tensor.matmul(out=xt[:, 2 + i % 2, :], lhsT=ident[:], rhs=ident[:], start=True, stop=True)
         for u in range(2):
             nc.tensor.transpose(xt[:, u, :], xw[:, u : D // 2 : 2], ident[:])
+        nc.gpsimd.tensor_copy(
+            out=b_pad[0:1, :].rearrange("o (u e g w) -> o u e g w", u=2, e=2, g=16, w=8),
+            in_=b_row[0:1, :].rearrange("o (g u w e) -> o u e g w", g=16, u=2, w=8, e=2),
+        )
+        bt = tpp.tile([P, 4, P], F32, name="bt", tag="tp")
+        for t in range(4):
+            nc.tensor.transpose(bt[:, t, :], b_pad[:, P * t : P * (t + 1)], ident[:])
+        for i in range(WARM1):
+            dummy(wt[:, i % 4, :])
         x_g = keep.tile([P, 4 * T], BF16, name="x_g", align_bytes=64)
         nc.vector.tensor_copy(
             out=x_g[:].bitcast(F32).rearrange("q (r u) -> q r u", u=2),
@@ -88,84 +119,133 @@ def tile_trittentioncube_pa_kernel(tc, normalized_resid_pre, W_C, b_C, W_K, out)
         x_codes = keep.tile([P, T], U32, name="x_codes", align_bytes=64)
         x_scales = keep.tile([P, T], U8, name="x_scales", align_bytes=64)
         nc.vector.quantize_mx(out=x_codes[:].bitcast(FP8X4), scales=x_scales[:], in_=x_g[:])
+        b_sb = keep.tile([P, 4], F32, name="b_sb")
+        nc.vector.tensor_copy(out=b_sb[:], in_=bt[:, :, 0])
 
         wc_g = keep.tile([P, 4 * KC], BF16, name="wc_g", align_bytes=64)
-        wc_dst = wc_g[:].rearrange("p (t n q j) -> p t n q j", t=4, n=NH, q=32, j=4)
-        wc_src = wc_raw[:].rearrange("p n (j q t) -> p t n q j", j=4, q=32, t=4)
+        wc_dst = wc_g[:].rearrange("p (u e n b w j) -> p u e n b w j", u=2, e=2, n=NH, b=4, w=8, j=4)
+        wc_src = wc_raw[:].rearrange("p n (j b u w e) -> p u e n b w j", j=4, b=4, u=2, w=8, e=2)
         for t in range(4):
             if t % 2 == 0:
-                nc.vector.tensor_copy(out=wc_dst[:, t], in_=wc_src[:, t])
+                nc.vector.tensor_copy(out=wc_dst[:, t // 2, t % 2], in_=wc_src[:, t // 2, t % 2])
             else:
-                nc.scalar.copy(out=wc_dst[:, t], in_=wc_src[:, t])
+                nc.scalar.copy(out=wc_dst[:, t // 2, t % 2], in_=wc_src[:, t // 2, t % 2])
         wc_codes = keep.tile([P, KC], U32, name="wc_codes", align_bytes=64)
         wc_scales = keep.tile([P, KC], U8, name="wc_scales", align_bytes=64)
-        nc.vector.quantize_mx(out=wc_codes[:].bitcast(FP8X4), scales=wc_scales[:], in_=wc_g[:])
-
-        c_ps = accp.tile([P, 4, T], BANK_DT, name="c_ps", tag="acc")
-        for t in range(4):
-            nc.tensor.matmul_mx(
-                out=c_ps[:, t, :],
-                lhsT=wc_codes[:, P * t : P * (t + 1)].bitcast(FP8X4),
-                lhsT_scale=wc_scales[:, P * t : P * (t + 1)],
-                rhs=x_codes[:].bitcast(FP8X4),
-                rhs_scale=x_scales[:],
-                start=True,
-                stop=True,
-            )
-        c_g = keep.tile([P, 4 * T], BF16, name="c_g", align_bytes=64)
-        nc.vector.tensor_tensor(
-            out=c_g[:].rearrange("q (r t) -> q r t", t=4),
-            in0=c_ps[:].rearrange("q t r -> q r t"),
-            in1=b_sb[:].unsqueeze(1).to_broadcast([P, T, 4]),
-            op=ADD,
-        )
         c_codes = keep.tile([P, T], U32, name="c_codes", align_bytes=64)
         c_scales = keep.tile([P, T], U8, name="c_scales", align_bytes=64)
-        nc.vector.quantize_mx(out=c_codes[:].bitcast(FP8X4), scales=c_scales[:], in_=c_g[:])
+        c_g = keep.tile([P, 4 * T], BF16, name="c_g", align_bytes=64)
+        c_ps = accp.tile([P, 4, T], BANK_DT, name="c_ps", tag="acc")
 
-        g = 0
-        for c, (raw, m, row0) in enumerate(raws):
-            raw_w = raw[:].rearrange("p n x -> p (n x)").bitcast(F32)
-            raw_v = raw_w.rearrange("p (n s w u) -> p s u n w", n=NH, s=m, w=32, u=2)
-            stg = stgp.tile([P, P * m], F32, name="stg", tag="stg")
-            stg_v = stg[:].rearrange("r (p s) -> r p s", s=m)
-            for sg in range(m // GS):
-                ordt = ordp.tile([P, GS, 2, P], F32, name="ordt", tag="ordt")
-                nc.vector.tensor_copy(
-                    out=ordt[:].rearrange("p s u (n w) -> p s u n w", n=NH),
-                    in_=raw_v[:, GS * sg : GS * (sg + 1), :, :, :],
-                )
-                grp = grpp.tile([P, 4 * 512], BF16, name="grp", tag="grp", align_bytes=64)
-                grp_w = grp[:].bitcast(F32)
-                for h in range(2):
-                    tp = tpp.tile([P, 4, P], F32, name="tp", tag="tp")
-                    if h == 0 or g < WARM_TWICE:
-                        nc.tensor.matmul(out=tp[:, 0, :], lhsT=ident[:], rhs=ident[:], start=True, stop=True)
-                    for a in range(4):
-                        nc.tensor.transpose(tp[:, a, :], ordt[:, 2 * h + a // 2, a % 2, :], ident[:])
-                    dst = grp_w[:, 512 * h : 512 * (h + 1)].rearrange("q (p a) -> q p a", a=4)
-                    src = tp[:].rearrange("q a p -> q p a")
-                    nc.scalar.copy(out=dst, in_=src)
-                codes = codp.tile([P, 512], U32, name="codes", tag="codes", align_bytes=64)
-                scales = codp.tile([P, 512], U8, name="scales", tag="scales", align_bytes=64)
-                nc.vector.quantize_mx(out=codes[:].bitcast(FP8X4), scales=scales[:], in_=grp[:])
-                acc = accp.tile([P, 512], F32, name="acc", tag="acc")
+        def stage1_products():
+            nc.vector.quantize_mx(out=wc_codes[:].bitcast(FP8X4), scales=wc_scales[:], in_=wc_g[:])
+            for t in range(4):
                 nc.tensor.matmul_mx(
-                    out=acc[:],
-                    lhsT=c_codes[:].bitcast(FP8X4),
-                    lhsT_scale=c_scales[:],
-                    rhs=codes[:].bitcast(FP8X4),
-                    rhs_scale=scales[:],
+                    out=c_ps[:, t, :],
+                    lhsT=wc_codes[:, P * t : P * (t + 1)].bitcast(FP8X4),
+                    lhsT_scale=wc_scales[:, P * t : P * (t + 1)],
+                    rhs=x_codes[:].bitcast(FP8X4),
+                    rhs_scale=x_scales[:],
                     start=True,
                     stop=True,
                 )
-                dst = stg_v[:, :, GS * sg : GS * (sg + 1)].rearrange("r p (h t) -> r p h t", h=2)
-                src = acc[:].rearrange("r (h p t) -> r p h t", h=2, t=2)
-                if g % 2 == 0:
+
+        def stage1_bias():
+            nc.vector.tensor_tensor(
+                out=c_g[:].rearrange("q (r t) -> q r t", t=4),
+                in0=c_ps[:].rearrange("q t r -> q r t"),
+                in1=b_sb[:].unsqueeze(1).to_broadcast([P, T, 4]),
+                op=ADD,
+            )
+            nc.vector.quantize_mx(out=c_codes[:].bitcast(FP8X4), scales=c_scales[:], in_=c_g[:])
+
+        ords = {}
+        tps = {}
+        grps = {}
+        cods = {}
+        accs = {}
+        stgs = {}
+
+        def reorder_and_transpose(g):
+            c, sg = group_chunk[g]
+            m = M_LIST[c]
+            raw_w = raws[c][:].rearrange("p n x -> p (n x)").bitcast(F32)
+            ordt = ordp.tile([P, GS, 2, P], F32, name="ordt", tag="ordt")
+            nc.vector.tensor_copy(
+                out=ordt[:].rearrange("p s u (n b w) -> p u n s b w", n=NH, b=4, w=8),
+                in_=raw_w.rearrange("p (n s b u w) -> p u n s b w", n=NH, s=m, b=4, u=2, w=8)[
+                    :, :, :, GS * sg : GS * (sg + 1), :, :
+                ],
+            )
+            pair = []
+            for h in range(2):
+                tp = tpp.tile([P, 4, P], F32, name="tp", tag="tp")
+                if h == 0 and g < WARM_TWICE:
+                    dummy(tp[:, 0, :])
+                for a in range(4):
+                    nc.tensor.transpose(tp[:, a, :], ordt[:, 2 * h + a // 2, a % 2, :], ident[:])
+                pair.append(tp)
+            tps[g] = pair
+
+        def copy_banks(g):
+            grp = grpp.tile([P, 4 * 512], BF16, name="grp", tag="grp", align_bytes=64)
+            grp_w = grp[:].bitcast(F32)
+            for h in range(2):
+                dst = grp_w[:, 512 * h : 512 * (h + 1)].rearrange("q (p a) -> q p a", a=4)
+                src = tps[g][h][:].rearrange("q a p -> q p a")
+                if h == 1 and g >= ng - 2:
                     nc.vector.tensor_copy(out=dst, in_=src)
                 else:
                     nc.scalar.copy(out=dst, in_=src)
-                g += 1
-            nc.sync.dma_start(out=out_dram[:, row0 : row0 + P * m], in_=stg[:])
-            for c2 in LOADS_AFTER_STORE.get(c, ()):
-                load(c2)
+            grps[g] = grp
+
+        def quantize_and_multiply(g):
+            codes = codp.tile([P, 512], U32, name="codes", tag="codes", align_bytes=64)
+            scales = codp.tile([P, 512], U8, name="scales", tag="scales", align_bytes=64)
+            nc.vector.quantize_mx(out=codes[:].bitcast(FP8X4), scales=scales[:], in_=grps[g][:])
+            acc = accp.tile([P, 512], F32, name="acc", tag="acc")
+            dummy(acc[:, 0:P])
+            nc.tensor.matmul_mx(
+                out=acc[:],
+                lhsT=c_codes[:].bitcast(FP8X4),
+                lhsT_scale=c_scales[:],
+                rhs=codes[:].bitcast(FP8X4),
+                rhs_scale=scales[:],
+                start=True,
+                stop=True,
+            )
+            accs[g] = acc
+
+        def copy_out_and_store(g):
+            c, sg = group_chunk[g]
+            m, row0, g0 = chunks[c]
+            if sg == 0:
+                stg_new = stgp.tile([P, P * m], F32, name="stg", tag="stg")
+                stgs[c] = stg_new
+            stg = stgs[c]
+            dst = stg[:].rearrange("r (p s) -> r p s", s=m)[:, :, GS * sg : GS * (sg + 1)].rearrange(
+                "r p (h t) -> r p h t", h=2
+            )
+            src = accs[g][:].rearrange("r (h p t) -> r p h t", h=2, t=2)
+            if (g + 1) * 2 // 5 > g * 2 // 5:
+                nc.vector.tensor_copy(out=dst, in_=src)
+            else:
+                nc.scalar.copy(out=dst, in_=src)
+            if sg == m // GS - 1:
+                nc.sync.dma_start(out=out_dram[:, row0 : row0 + P * m], in_=stg[:])
+
+        for i in range(ng + LAG_D):
+            if i > 0:
+                loads_of_step(i)
+            if 0 <= i - LAG_Q < ng:
+                quantize_and_multiply(i - LAG_Q)
+            if i == 0:
+                stage1_products()
+            if i == 1:
+                stage1_bias()
+            if 0 <= i - LAG_B < ng:
+                copy_banks(i - LAG_B)
+            if i < ng:
+                reorder_and_transpose(i)
+            if 0 <= i - LAG_D < ng:
+                copy_out_and_store(i - LAG_D)

@@ -20,9 +20,9 @@ ROWS = DH * DH
 FLOPS = 2 * T * D * KC + 2 * T * KC * ROWS
 
 BANK_DT = F32
-M_LIST = [4,4,4,4,8,8,16,16,16,16,16,8,4,4]
+M_LIST = [4,8,8,12,16,16,16,16,16,8,4,4]
 GS = 4
-LEAD = 6
+LEAD = 8
 LAG_B = 2
 LAG_Q = 3
 LAG_D = 4
@@ -80,12 +80,12 @@ def tile_trittentioncube_pa_kernel(tc, normalized_resid_pre, W_C, b_C, W_K, out)
         def dummy(dst):
             nc.tensor.matmul(out=dst, lhsT=ident[:], rhs=ident[:], start=True, stop=True)
 
+        b_row = keep.tile([1, KC], BF16, name="b_row")
+        nc.sync.dma_start(out=b_row[:], in_=b_C.rearrange("(o n) k -> o (n k)", o=1))
         x_sb = keep.tile([P, D], BF16, name="x_sb")
         nc.sync.dma_start(out=x_sb[:], in_=x_dram)
         wc_raw = keep.tile([P, NH, 4 * DH], BF16, name="wc_raw")
         nc.sync.dma_start(out=wc_raw[:], in_=W_C.rearrange("n (p j) k -> p n (j k)", j=4))
-        b_row = keep.tile([1, KC], BF16, name="b_row")
-        nc.sync.dma_start(out=b_row[:], in_=b_C.rearrange("(o n) k -> o (n k)", o=1))
         loads_of_step(0)
 
         ident = keep.tile([P, P], F32, name="ident")
@@ -120,7 +120,6 @@ def tile_trittentioncube_pa_kernel(tc, normalized_resid_pre, W_C, b_C, W_K, out)
         x_scales = keep.tile([P, T], U8, name="x_scales", align_bytes=64)
         nc.vector.quantize_mx(out=x_codes[:].bitcast(FP8X4), scales=x_scales[:], in_=x_g[:])
         b_sb = keep.tile([P, 4], F32, name="b_sb")
-        nc.vector.tensor_copy(out=b_sb[:], in_=bt[:, :, 0])
 
         wc_g = keep.tile([P, 4 * KC], BF16, name="wc_g", align_bytes=64)
         wc_dst = wc_g[:].rearrange("p (u e n b w j) -> p u e n b w j", u=2, e=2, n=NH, b=4, w=8, j=4)
@@ -151,6 +150,7 @@ def tile_trittentioncube_pa_kernel(tc, normalized_resid_pre, W_C, b_C, W_K, out)
                 )
 
         def stage1_bias():
+            nc.vector.tensor_copy(out=b_sb[:], in_=bt[:, :, 0])
             nc.vector.tensor_tensor(
                 out=c_g[:].rearrange("q (r t) -> q r t", t=4),
                 in0=c_ps[:].rearrange("q t r -> q r t"),
@@ -193,10 +193,7 @@ def tile_trittentioncube_pa_kernel(tc, normalized_resid_pre, W_C, b_C, W_K, out)
             for h in range(2):
                 dst = grp_w[:, 512 * h : 512 * (h + 1)].rearrange("q (p a) -> q p a", a=4)
                 src = tps[g][h][:].rearrange("q a p -> q p a")
-                if h == 1 and g >= ng - 2:
-                    nc.vector.tensor_copy(out=dst, in_=src)
-                else:
-                    nc.scalar.copy(out=dst, in_=src)
+                nc.scalar.copy(out=dst, in_=src)
             grps[g] = grp
 
         def quantize_and_multiply(g):
@@ -227,7 +224,7 @@ def tile_trittentioncube_pa_kernel(tc, normalized_resid_pre, W_C, b_C, W_K, out)
                 "r p (h t) -> r p h t", h=2
             )
             src = accs[g][:].rearrange("r (h p t) -> r p h t", h=2, t=2)
-            if (g + 1) * 2 // 5 > g * 2 // 5:
+            if (g + 1) * 9 // 20 > g * 9 // 20:
                 nc.vector.tensor_copy(out=dst, in_=src)
             else:
                 nc.scalar.copy(out=dst, in_=src)

from contextlib import ExitStack

import concourse.mybir as mybir
from concourse.masks import make_identity

F32 = mybir.dt.float32
BF16 = mybir.dt.bfloat16
U32 = mybir.dt.uint32
U8 = mybir.dt.uint8
FP8X4 = mybir.dt.float8_e4m3fn_x4
ADD = mybir.AluOpType.add

P = 128
T = 128
D = 512
NH = 4
DH = 128
KC = NH * DH
ROWS = DH * DH
FLOPS = 2 * T * D * KC + 2 * T * KC * ROWS

BANK_DT = F32
M_LIST = [4,8,8,12,16,16,16,16,16,8,4,4]
GS = 4
LEAD = 8
LAG_B = 2
LAG_Q = 3
LAG_D = 4
WARM0 = 2
WARM1 = 4
WARM_TWICE = 8


def tile_trittentioncube_pa_kernel(tc, normalized_resid_pre, W_C, b_C, W_K, out):
    nc = tc.nc
    assert sum(M_LIST) == DH
    x_dram = normalized_resid_pre.rearrange("b r d -> (b r) d")
    out_dram = out.rearrange("b r i j -> (b r) (i j)")
    wk_dram = W_K.rearrange("n i j k -> n (i j) k")

    chunks = []
    group_chunk = []
    row0 = 0
    for c, m in enumerate(M_LIST):
        chunks.append((m, row0, len(group_chunk)))
        for sg in range(m // GS):
            group_chunk.append((c, sg))
        row0 += P * m
    ng = len(group_chunk)

    with ExitStack() as ctx:
        keep = ctx.enter_context(tc.tile_pool(name="keep", bufs=1))
        rawp = ctx.enter_context(tc.tile_pool(name="rawp", bufs=1))
        ordp = ctx.enter_context(tc.tile_pool(name="ordp", bufs=3))
        grpp = ctx.enter_context(tc.tile_pool(name="grpp", bufs=3))
        codp = ctx.enter_context(tc.tile_pool(name="codp", bufs=3))
        stgp = ctx.enter_context(tc.tile_pool(name="stgp", bufs=4))
        tpp = ctx.enter_context(tc.psum_pool(name="tpp", bufs=6))
        accp = ctx.enter_context(tc.psum_pool(name="accp", bufs=2))
        ctx.enter_context(tc.manual_schedule())

        raws = []
        for c, m in enumerate(M_LIST):
            raw = rawp.tile([P, NH, m * DH], BF16, name="raw%d" % c)
            raws.append(raw)

        def load(c):
            m, row0, g0 = chunks[c]
            nc.sync.dma_start(
                out=raws[c][:],
                in_=wk_dram[:, row0 : row0 + P * m, :].rearrange("n (p s) k -> p n (s k)", s=m),
            )

        def loads_of_step(i):
            for c in range(len(chunks)):
                first = max(chunks[c][2] - LEAD, 0)
                if first == i:
                    load(c)

        def dummy(dst):
            nc.tensor.matmul(out=dst, lhsT=ident[:], rhs=ident[:], start=True, stop=True)

        b_row = keep.tile([1, KC], BF16, name="b_row")
        nc.sync.dma_start(out=b_row[:], in_=b_C.rearrange("(o n) k -> o (n k)", o=1))
        x_sb = keep.tile([P, D], BF16, name="x_sb")
        nc.sync.dma_start(out=x_sb[:], in_=x_dram)
        wc_raw = keep.tile([P, NH, 4 * DH], BF16, name="wc_raw")
        nc.sync.dma_start(out=wc_raw[:], in_=W_C.rearrange("n (p j) k -> p n (j k)", j=4))
        loads_of_step(0)

        ident = keep.tile([P, P], F32, name="ident")
        make_identity(nc, ident[:])
        b_pad = keep.tile([P, KC], F32, name="b_pad")
        nc.gpsimd.memset(b_pad[:], 0.0)
        warm = keep.tile([P, 8], F32, name="warm")
        nc.scalar.copy(out=warm[:], in_=ident[:, 0:8])

        wt = tpp.tile([P, 4, P], F32, name="wt", tag="tp")
        for i in range(WARM0):
            dummy(wt[:, i % 4, :])
        xw = x_sb[:].bitcast(F32)
        xt = tpp.tile([P, 4, P], F32, name="xt", tag="tp")
        for u in range(2):
            nc.tensor.transpose(xt[:, u, :], xw[:, u : D // 2 : 2], ident[:])
        nc.gpsimd.tensor_copy(
            out=b_pad[0:1, :].rearrange("o (u e g w) -> o u e g w", u=2, e=2, g=16, w=8),
            in_=b_row[0:1, :].rearrange("o (g u w e) -> o u e g w", g=16, u=2, w=8, e=2),
        )
        bt = tpp.tile([P, 4, P], F32, name="bt", tag="tp")
        for t in range(4):
            nc.tensor.transpose(bt[:, t, :], b_pad[:, P * t : P * (t + 1)], ident[:])
        for i in range(WARM1):
            dummy(wt[:, i % 4, :])
        x_g = keep.tile([P, 4 * T], BF16, name="x_g", align_bytes=64)
        nc.vector.tensor_copy(
            out=x_g[:].bitcast(F32).rearrange("q (r u) -> q r u", u=2),
            in_=xt[:, 0:2, :].rearrange("q u r -> q r u"),
        )
        x_codes = keep.tile([P, T], U32, name="x_codes", align_bytes=64)
        x_scales = keep.tile([P, T], U8, name="x_scales", align_bytes=64)
        nc.vector.quantize_mx(out=x_codes[:].bitcast(FP8X4), scales=x_scales[:], in_=x_g[:])
        b_sb = keep.tile([P, 4], F32, name="b_sb")

        wc_g = keep.tile([P, 4 * KC], BF16, name="wc_g", align_bytes=64)
        wc_dst = wc_g[:].rearrange("p (u e n b w j) -> p u e n b w j", u=2, e=2, n=NH, b=4, w=8, j=4)
        wc_src = wc_raw[:].rearrange("p n (j b u w e) -> p u e n b w j", j=4, b=4, u=2, w=8, e=2)
        for t in range(4):
            if t % 2 == 0:
                nc.vector.tensor_copy(out=wc_dst[:, t // 2, t % 2], in_=wc_src[:, t // 2, t % 2])
            else:
                nc.scalar.copy(out=wc_dst[:, t // 2, t % 2], in_=wc_src[:, t // 2, t % 2])
        wc_codes = keep.tile([P, KC], U32, name="wc_codes", align_bytes=64)
        wc_scales = keep.tile([P, KC], U8, name="wc_scales", align_bytes=64)
        c_codes = keep.tile([P, T], U32, name="c_codes", align_bytes=64)
        c_scales = keep.tile([P, T], U8, name="c_scales", align_bytes=64)
        c_g = keep.tile([P, 4 * T], BF16, name="c_g", align_bytes=64)
        c_ps = accp.tile([P, 4, T], BANK_DT, name="c_ps", tag="acc")

        def stage1_products():
            nc.vector.quantize_mx(out=wc_codes[:].bitcast(FP8X4), scales=wc_scales[:], in_=wc_g[:])
            for t in range(4):
                nc.tensor.matmul_mx(
                    out=c_ps[:, t, :],
                    lhsT=wc_codes[:, P * t : P * (t + 1)].bitcast(FP8X4),
                    lhsT_scale=wc_scales[:, P * t : P * (t + 1)],
                    rhs=x_codes[:].bitcast(FP8X4),
                    rhs_scale=x_scales[:],
                    start=True,
                    stop=True,
                )

        def stage1_bias():
            nc.vector.tensor_copy(out=b_sb[:], in_=bt[:, :, 0])
            nc.vector.tensor_tensor(
                out=c_g[:].rearrange("q (r t) -> q r t", t=4),
                in0=c_ps[:].rearrange("q t r -> q r t"),
                in1=b_sb[:].unsqueeze(1).to_broadcast([P, T, 4]),
                op=ADD,
            )
            nc.vector.quantize_mx(out=c_codes[:].bitcast(FP8X4), scales=c_scales[:], in_=c_g[:])

        ords = {}
        tps = {}
        grps = {}
        cods = {}
        accs = {}
        stgs = {}

        def reorder_and_transpose(g):
            c, sg = group_chunk[g]
            m = M_LIST[c]
            raw_w = raws[c][:].rearrange("p n x -> p (n x)").bitcast(F32)
            ordt = ordp.tile([P, GS, 2, P], F32, name="ordt", tag="ordt")
            nc.vector.tensor_copy(
                out=ordt[:].rearrange("p s u (n b w) -> p u n s b w", n=NH, b=4, w=8),
                in_=raw_w.rearrange("p (n s b u w) -> p u n s b w", n=NH, s=m, b=4, u=2, w=8)[
                    :, :, :, GS * sg : GS * (sg + 1), :, :
                ],
            )
            pair = []
            for h in range(2):
                tp = tpp.tile([P, 4, P], F32, name="tp", tag="tp")
                if h == 0 and g < WARM_TWICE:
                    dummy(tp[:, 0, :])
                for a in range(4):
                    nc.tensor.transpose(tp[:, a, :], ordt[:, 2 * h + a // 2, a % 2, :], ident[:])
                pair.append(tp)
            tps[g] = pair

        def copy_banks(g):
            grp = grpp.tile([P, 4 * 512], BF16, name="grp", tag="grp", align_bytes=64)
            grp_w = grp[:].bitcast(F32)
            for h in range(2):
                dst = grp_w[:, 512 * h : 512 * (h + 1)].rearrange("q (p a) -> q p a", a=4)
                src = tps[g][h][:].rearrange("q a p -> q p a")
                nc.scalar.copy(out=dst, in_=src)
            grps[g] = grp

        def quantize_and_multiply(g):
            codes = codp.tile([P, 512], U32, name="codes", tag="codes", align_bytes=64)
            scales = codp.tile([P, 512], U8, name="scales", tag="scales", align_bytes=64)
            nc.vector.quantize_mx(out=codes[:].bitcast(FP8X4), scales=scales[:], in_=grps[g][:])
            acc = accp.tile([P, 512], F32, name="acc", tag="acc")
            dummy(acc[:, 0:P])
            nc.tensor.matmul_mx(
                out=acc[:],
                lhsT=c_codes[:].bitcast(FP8X4),
                lhsT_scale=c_scales[:],
                rhs=codes[:].bitcast(FP8X4),
                rhs_scale=scales[:],
                start=True,
                stop=True,
            )
            accs[g] = acc

        def copy_out_and_store(g):
            c, sg = group_chunk[g]
            m, row0, g0 = chunks[c]
            if sg == 0:
                stg_new = stgp.tile([P, P * m], F32, name="stg", tag="stg")
                stgs[c] = stg_new
            stg = stgs[c]
            dst = stg[:].rearrange("r (p s) -> r p s", s=m)[:, :, GS * sg : GS * (sg + 1)].rearrange(
                "r p (h t) -> r p h t", h=2
            )
            src = accs[g][:].rearrange("r (h p t) -> r p h t", h=2, t=2)
            if (g + 1) * 9 // 20 > g * 9 // 20:
                nc.vector.tensor_copy(out=dst, in_=src)
            else:
                nc.scalar.copy(out=dst, in_=src)
            if sg == m // GS - 1:
                nc.sync.dma_start(out=out_dram[:, row0 : row0 + P * m], in_=stg[:])

        for i in range(ng + LAG_D):
            if i > 0:
                loads_of_step(i)
            if 0 <= i - LAG_Q < ng:
                quantize_and_multiply(i - LAG_Q)
            if i == 0:
                stage1_products()
            if i == 1:
                stage1_bias()
            if 0 <= i - LAG_B < ng:
                copy_banks(i - LAG_B)
            if i < ng:
                reorder_and_transpose(i)
            if 0 <= i - LAG_D < ng:
                copy_out_and_store(i - LAG_D)
